import numpy as np
import ml_dtypes

BF16 = ml_dtypes.bfloat16


def bf(x):
    return np.asarray(x, np.float32).astype(BF16)


def f32(x):
    return np.asarray(x, np.float32)


def f64(x):
    return np.asarray(x).astype(np.float64)


def striped(idx):
    return np.tile(idx.reshape(-1, 16).T, (8, 1))


D, S, N, NH, NKV, HD, HALF, M = 128, 4096, 1024, 2, 1, 128, 64, 512
ROPE_BASE = 10000.0


def rope_tables():
    p = f32(ROPE_BASE ** (np.arange(HALF) / HALF))
    inv = f32(1.0) / p
    t = f32(np.arange(N))
    ang = inv[:, None] * t[None, :]
    emb = np.concatenate([ang, ang], axis=0)
    return f32(np.cos(f64(emb))), f32(np.sin(f64(emb)))


def setup_inputs():
    cos_t, sin_t = rope_tables()
    return {"table": bf(np.random.standard_normal((D, S))), "w": bf(np.random.standard_normal((D, M)) / np.sqrt(D)), "cos_t": cos_t, "sin_t": sin_t, "offs": striped(np.random.permutation(S)[:N])}


def reference(table, w, cos_t, sin_t, offs):
    idx = offs[:16].T.reshape(-1)
    y = f64(w).T @ f64(table)[:, idx]
    q = y[:NH * HD].reshape(NH, HD, N)
    rot = np.concatenate([-q[:, HALF:], q[:, :HALF]], axis=1)
    qr = q * f64(cos_t)[None] + rot * f64(sin_t)[None]
    return np.concatenate([qr.reshape(NH * HD, N), y[NH * HD:]], axis=0)

@@ -1,0 +1,74 @@
+import concourse.mybir as mybir
+
+BF16, F32, U16 = mybir.dt.bfloat16, mybir.dt.float32, mybir.dt.uint16
+MULT, ADD = mybir.AluOpType.mult, mybir.AluOpType.add
+COPY = mybir.ActivationFunctionType.Copy
+
+P = 128
+S = 4096
+N = 1024
+M = 512
+HEADS_Q = 2
+HALF = P // 2
+PIECE = 512
+PIECES = N // PIECE
+PIECE_COLS = PIECE // 16
+
+FLOPS = 2 * P * M * N
+
+
+def tile_compressedllamaattention_kernel(tc, table, w, cos_t, sin_t, offs, out):
+    nc = tc.nc
+    with (
+        tc.tile_pool(name="held", bufs=1) as held,
+        tc.tile_pool(name="work", bufs=4) as work,
+        tc.psum_pool(name="psum", bufs=8) as psum,
+    ):
+        offsets = held.tile([P, N // 16], U16, name="offsets")
+        nc.sync.dma_start(offsets[:], offs)
+        weights = held.tile([P, M], BF16, name="weights")
+        nc.scalar.dma_start(weights[:], w)
+        tokens = held.tile([P, S], BF16, name="tokens")
+        nc.sync.dma_start(tokens[:, : S // 2], table[:, : S // 2])
+        nc.scalar.dma_start(tokens[:, S // 2 :], table[:, S // 2 :])
+        cosines = held.tile([P, N], F32, name="cosines")
+        sines = held.tile([P, N], F32, name="sines")
+        for p in range(PIECES):
+            cols = slice(p * PIECE, (p + 1) * PIECE)
+            nc.sync.dma_start(cosines[:, cols], cos_t[:, cols])
+            nc.scalar.dma_start(sines[:, cols], sin_t[:, cols])
+
+        partner_weights = held.tile([P, HEADS_Q * P], BF16, name="partner_weights")
+        for h in range(HEADS_Q):
+            lo, mid, hi = h * P, h * P + HALF, (h + 1) * P
+            nc.vector.tensor_scalar_mul(partner_weights[:, lo:mid], weights[:, mid:hi], -1.0)
+            nc.vector.tensor_copy(partner_weights[:, mid:hi], weights[:, lo:mid])
+
+        def looked_up(p):
+            return tokens[:].indirect(offsets[:, p * PIECE_COLS : (p + 1) * PIECE_COLS])
+
+        for p in range(PIECES):
+            cols = slice(p * PIECE, (p + 1) * PIECE)
+            for h in range(HEADS_Q):
+                rows = slice(h * P, (h + 1) * P)
+                y = psum.tile([P, PIECE], F32, name="y", tag="bank")
+                nc.tensor.matmul(y[:], weights[:, rows], looked_up(p), start=True, stop=True)
+                partner = psum.tile([P, PIECE], F32, name="partner", tag="bank")
+                nc.tensor.matmul(partner[:], partner_weights[:, rows], looked_up(p), start=True, stop=True)
+                y_cos = work.tile([P, PIECE], F32, name="y_cos")
+                nc.vector.tensor_tensor(y_cos[:], y[:], cosines[:, cols], MULT)
+                partner_sin = work.tile([P, PIECE], F32, name="partner_sin")
+                nc.vector.tensor_tensor(partner_sin[:], partner[:], sines[:, cols], MULT)
+                rotated = work.tile([P, PIECE], F32, name="rotated")
+                nc.gpsimd.tensor_tensor(rotated[:], y_cos[:], partner_sin[:], ADD)
+                nc.sync.dma_start(out[rows, cols], rotated[:])
+
+        for p in range(PIECES):
+            cols = slice(p * PIECE, (p + 1) * PIECE)
+            for m in range(HEADS_Q, M // P):
+                rows = slice(m * P, (m + 1) * P)
+                y = psum.tile([P, PIECE], F32, name="y", tag="bank")
+                nc.tensor.matmul(y[:], weights[:, rows], looked_up(p), start=True, stop=True)
+                plain = work.tile([P, PIECE], F32, name="plain")
+                nc.scalar.activation(plain[:], y[:], COPY)
+                nc.scalar.dma_start(out[rows, cols], plain[:])

@@ -1,7 +1,7 @@
 import concourse.mybir as mybir
 
 BF16, F32, U16 = mybir.dt.bfloat16, mybir.dt.float32, mybir.dt.uint16
-MULT, ADD = mybir.AluOpType.mult, mybir.AluOpType.add
+MULT, ADD, SUBTRACT = mybir.AluOpType.mult, mybir.AluOpType.add, mybir.AluOpType.subtract
 COPY = mybir.ActivationFunctionType.Copy
 
 P = 128
@@ -31,44 +31,57 @@ def tile_compressedllamaattention_kernel(tc, table, w, cos_t, sin_t, offs, out):
         tokens = held.tile([P, S], BF16, name="tokens")
         nc.sync.dma_start(tokens[:, : S // 2], table[:, : S // 2])
         nc.scalar.dma_start(tokens[:, S // 2 :], table[:, S // 2 :])
-        cosines = held.tile([P, N], F32, name="cosines")
-        sines = held.tile([P, N], F32, name="sines")
+
+        LOW, HIGH = 0, 1
+        pair_weights = [held.tile([P, P], BF16, name=f"pair_weights{t}") for t in (LOW, HIGH)]
+        for t in (LOW, HIGH):
+            for h in range(HEADS_Q):
+                nc.vector.tensor_copy(
+                    pair_weights[t][:, h * HALF : (h + 1) * HALF],
+                    weights[:, h * P + t * HALF : h * P + (t + 1) * HALF],
+                )
+        cosines = [held.tile([P, N], F32, name=f"cosines{t}") for t in (LOW, HIGH)]
+        sines = [held.tile([P, N], F32, name=f"sines{t}") for t in (LOW, HIGH)]
+        queue_of_head = (nc.sync, nc.scalar)
         for p in range(PIECES):
             cols = slice(p * PIECE, (p + 1) * PIECE)
-            nc.sync.dma_start(cosines[:, cols], cos_t[:, cols])
-            nc.scalar.dma_start(sines[:, cols], sin_t[:, cols])
-
-        partner_weights = held.tile([P, HEADS_Q * P], BF16, name="partner_weights")
-        for h in range(HEADS_Q):
-            lo, mid, hi = h * P, h * P + HALF, (h + 1) * P
-            nc.vector.tensor_scalar_mul(partner_weights[:, lo:mid], weights[:, mid:hi], -1.0)
-            nc.vector.tensor_copy(partner_weights[:, mid:hi], weights[:, lo:mid])
+            for t in (LOW, HIGH):
+                for tile_sb, dram in ((cosines[t], cos_t), (sines[t], sin_t)):
+                    for h in range(HEADS_Q):
+                        queue_of_head[h].dma_start(
+                            tile_sb[h * HALF : (h + 1) * HALF, cols],
+                            dram[t * HALF : (t + 1) * HALF, cols],
+                        )
 
         def looked_up(p):
             return tokens[:].indirect(offsets[:, p * PIECE_COLS : (p + 1) * PIECE_COLS])
 
         for p in range(PIECES):
             cols = slice(p * PIECE, (p + 1) * PIECE)
-            for h in range(HEADS_Q):
-                rows = slice(h * P, (h + 1) * P)
-                y = psum.tile([P, PIECE], F32, name="y", tag="bank")
-                nc.tensor.matmul(y[:], weights[:, rows], looked_up(p), start=True, stop=True)
-                partner = psum.tile([P, PIECE], F32, name="partner", tag="bank")
-                nc.tensor.matmul(partner[:], partner_weights[:, rows], looked_up(p), start=True, stop=True)
-                y_cos = work.tile([P, PIECE], F32, name="y_cos")
-                nc.vector.tensor_tensor(y_cos[:], y[:], cosines[:, cols], MULT)
-                partner_sin = work.tile([P, PIECE], F32, name="partner_sin")
-                nc.vector.tensor_tensor(partner_sin[:], partner[:], sines[:, cols], MULT)
+            y = []
+            for t in (LOW, HIGH):
+                y.append(psum.tile([P, PIECE], F32, name=f"y{t}", tag="bank"))
+                nc.tensor.matmul(y[t][:], pair_weights[t][:], looked_up(p), start=True, stop=True)
+            for t in (LOW, HIGH):
+                own_cos = work.tile([P, PIECE], F32, name="own_cos")
+                nc.vector.tensor_tensor(own_cos[:], y[t][:], cosines[t][:, cols], MULT)
+                other_sin = work.tile([P, PIECE], F32, name="other_sin")
+                nc.vector.tensor_tensor(other_sin[:], y[1 - t][:], sines[t][:, cols], MULT)
                 rotated = work.tile([P, PIECE], F32, name="rotated")
-                nc.gpsimd.tensor_tensor(rotated[:], y_cos[:], partner_sin[:], ADD)
-                nc.sync.dma_start(out[rows, cols], rotated[:])
+                combiner = nc.vector if (p == PIECES - 1 and t == HIGH) else nc.gpsimd
+                combiner.tensor_tensor(rotated[:], own_cos[:], other_sin[:], SUBTRACT if t == LOW else ADD)
+                for h in range(HEADS_Q):
+                    nc.sync.dma_start(
+                        out[h * P + t * HALF : h * P + (t + 1) * HALF, cols],
+                        rotated[h * HALF : (h + 1) * HALF, :],
+                    )
 
         for p in range(PIECES):
             cols = slice(p * PIECE, (p + 1) * PIECE)
             for m in range(HEADS_Q, M // P):
                 rows = slice(m * P, (m + 1) * P)
-                y = psum.tile([P, PIECE], F32, name="y", tag="bank")
-                nc.tensor.matmul(y[:], weights[:, rows], looked_up(p), start=True, stop=True)
+                y_plain = psum.tile([P, PIECE], F32, name="y_plain", tag="bank")
+                nc.tensor.matmul(y_plain[:], weights[:, rows], looked_up(p), start=True, stop=True)
                 plain = work.tile([P, PIECE], F32, name="plain")
-                nc.scalar.activation(plain[:], y[:], COPY)
+                nc.scalar.activation(plain[:], y_plain[:], COPY)
                 nc.scalar.dma_start(out[rows, cols], plain[:])

@@ -1,7 +1,7 @@
 import concourse.mybir as mybir
 
 BF16, F32, U16 = mybir.dt.bfloat16, mybir.dt.float32, mybir.dt.uint16
-MULT, ADD, SUBTRACT = mybir.AluOpType.mult, mybir.AluOpType.add, mybir.AluOpType.subtract
+MULT, ADD = mybir.AluOpType.mult, mybir.AluOpType.add
 COPY = mybir.ActivationFunctionType.Copy
 
 P = 128
@@ -13,6 +13,7 @@ HALF = P // 2
 PIECE = 512
 PIECES = N // PIECE
 PIECE_COLS = PIECE // 16
+WARM_UP = 12
 
 FLOPS = 2 * P * M * N
 
@@ -31,57 +32,50 @@ def tile_compressedllamaattention_kernel(tc, table, w, cos_t, sin_t, offs, out):
         tokens = held.tile([P, S], BF16, name="tokens")
         nc.sync.dma_start(tokens[:, : S // 2], table[:, : S // 2])
         nc.scalar.dma_start(tokens[:, S // 2 :], table[:, S // 2 :])
-
-        LOW, HIGH = 0, 1
-        pair_weights = [held.tile([P, P], BF16, name=f"pair_weights{t}") for t in (LOW, HIGH)]
-        for t in (LOW, HIGH):
-            for h in range(HEADS_Q):
-                nc.vector.tensor_copy(
-                    pair_weights[t][:, h * HALF : (h + 1) * HALF],
-                    weights[:, h * P + t * HALF : h * P + (t + 1) * HALF],
-                )
-        cosines = [held.tile([P, N], F32, name=f"cosines{t}") for t in (LOW, HIGH)]
-        sines = [held.tile([P, N], F32, name=f"sines{t}") for t in (LOW, HIGH)]
-        queue_of_head = (nc.sync, nc.scalar)
+        cosines = held.tile([P, N], F32, name="cosines")
+        sines = held.tile([P, N], F32, name="sines")
         for p in range(PIECES):
             cols = slice(p * PIECE, (p + 1) * PIECE)
-            for t in (LOW, HIGH):
-                for tile_sb, dram in ((cosines[t], cos_t), (sines[t], sin_t)):
-                    for h in range(HEADS_Q):
-                        queue_of_head[h].dma_start(
-                            tile_sb[h * HALF : (h + 1) * HALF, cols],
-                            dram[t * HALF : (t + 1) * HALF, cols],
-                        )
+            nc.sync.dma_start(cosines[:, cols], cos_t[:, cols])
+            nc.scalar.dma_start(sines[:, cols], sin_t[:, cols])
+
+        zeros = held.tile([P, PIECE], BF16, name="zeros")
+        nc.vector.memset(zeros[:], 0.0)
+        unused = psum.tile([P, PIECE], F32, name="unused", tag="bank")
+        for i in range(WARM_UP):
+            nc.tensor.matmul(unused[:], zeros[:, :P], zeros[:], start=True, stop=True)
+
+        partner_weights = held.tile([P, HEADS_Q * P], BF16, name="partner_weights")
+        for h in range(HEADS_Q):
+            lo, mid, hi = h * P, h * P + HALF, (h + 1) * P
+            nc.vector.tensor_scalar_mul(partner_weights[:, lo:mid], weights[:, mid:hi], -1.0)
+            nc.vector.tensor_copy(partner_weights[:, mid:hi], weights[:, lo:mid])
 
         def looked_up(p):
             return tokens[:].indirect(offsets[:, p * PIECE_COLS : (p + 1) * PIECE_COLS])
 
         for p in range(PIECES):
             cols = slice(p * PIECE, (p + 1) * PIECE)
-            y = []
-            for t in (LOW, HIGH):
-                y.append(psum.tile([P, PIECE], F32, name=f"y{t}", tag="bank"))
-                nc.tensor.matmul(y[t][:], pair_weights[t][:], looked_up(p), start=True, stop=True)
-            for t in (LOW, HIGH):
-                own_cos = work.tile([P, PIECE], F32, name="own_cos")
-                nc.vector.tensor_tensor(own_cos[:], y[t][:], cosines[t][:, cols], MULT)
-                other_sin = work.tile([P, PIECE], F32, name="other_sin")
-                nc.vector.tensor_tensor(other_sin[:], y[1 - t][:], sines[t][:, cols], MULT)
+            for h in range(HEADS_Q):
+                rows = slice(h * P, (h + 1) * P)
+                y = psum.tile([P, PIECE], F32, name="y", tag="bank")
+                nc.tensor.matmul(y[:], weights[:, rows], looked_up(p), start=True, stop=True)
+                partner = psum.tile([P, PIECE], F32, name="partner", tag="bank")
+                nc.tensor.matmul(partner[:], partner_weights[:, rows], looked_up(p), start=True, stop=True)
+                y_cos = work.tile([P, PIECE], F32, name="y_cos")
+                nc.vector.tensor_tensor(y_cos[:], y[:], cosines[:, cols], MULT)
+                partner_sin = work.tile([P, PIECE], F32, name="partner_sin")
+                nc.vector.tensor_tensor(partner_sin[:], partner[:], sines[:, cols], MULT)
                 rotated = work.tile([P, PIECE], F32, name="rotated")
-                combiner = nc.vector if (p == PIECES - 1 and t == HIGH) else nc.gpsimd
-                combiner.tensor_tensor(rotated[:], own_cos[:], other_sin[:], SUBTRACT if t == LOW else ADD)
-                for h in range(HEADS_Q):
-                    nc.sync.dma_start(
-                        out[h * P + t * HALF : h * P + (t + 1) * HALF, cols],
-                        rotated[h * HALF : (h + 1) * HALF, :],
-                    )
+                nc.gpsimd.tensor_tensor(rotated[:], y_cos[:], partner_sin[:], ADD)
+                nc.sync.dma_start(out[rows, cols], rotated[:])
 
         for p in range(PIECES):
             cols = slice(p * PIECE, (p + 1) * PIECE)
             for m in range(HEADS_Q, M // P):
                 rows = slice(m * P, (m + 1) * P)
-                y_plain = psum.tile([P, PIECE], F32, name="y_plain", tag="bank")
-                nc.tensor.matmul(y_plain[:], weights[:, rows], looked_up(p), start=True, stop=True)
+                y = psum.tile([P, PIECE], F32, name="y", tag="bank")
+                nc.tensor.matmul(y[:], weights[:, rows], looked_up(p), start=True, stop=True)
                 plain = work.tile([P, PIECE], F32, name="plain")
-                nc.scalar.activation(plain[:], y_plain[:], COPY)
+                nc.scalar.activation(plain[:], y[:], COPY)
                 nc.scalar.dma_start(out[rows, cols], plain[:])

@@ -13,7 +13,6 @@ HALF = P // 2
 PIECE = 512
 PIECES = N // PIECE
 PIECE_COLS = PIECE // 16
-WARM_UP = 12
 
 FLOPS = 2 * P * M * N
 
@@ -38,12 +37,6 @@ def tile_compressedllamaattention_kernel(tc, table, w, cos_t, sin_t, offs, out):
             cols = slice(p * PIECE, (p + 1) * PIECE)
             nc.sync.dma_start(cosines[:, cols], cos_t[:, cols])
             nc.scalar.dma_start(sines[:, cols], sin_t[:, cols])
-
-        zeros = held.tile([P, PIECE], BF16, name="zeros")
-        nc.vector.memset(zeros[:], 0.0)
-        unused = psum.tile([P, PIECE], F32, name="unused", tag="bank")
-        for i in range(WARM_UP):
-            nc.tensor.matmul(unused[:], zeros[:, :P], zeros[:], start=True, stop=True)
 
         partner_weights = held.tile([P, HEADS_Q * P], BF16, name="partner_weights")
         for h in range(HEADS_Q):
@@ -70,12 +63,17 @@ def tile_compressedllamaattention_kernel(tc, table, w, cos_t, sin_t, offs, out):
                 nc.gpsimd.tensor_tensor(rotated[:], y_cos[:], partner_sin[:], ADD)
                 nc.sync.dma_start(out[rows, cols], rotated[:])
 
+        KEY, VALUE = HEADS_Q, HEADS_Q + 1
         for p in range(PIECES):
             cols = slice(p * PIECE, (p + 1) * PIECE)
-            for m in range(HEADS_Q, M // P):
+            for m in (KEY, VALUE):
                 rows = slice(m * P, (m + 1) * P)
                 y = psum.tile([P, PIECE], F32, name="y", tag="bank")
                 nc.tensor.matmul(y[:], weights[:, rows], looked_up(p), start=True, stop=True)
                 plain = work.tile([P, PIECE], F32, name="plain")
-                nc.scalar.activation(plain[:], y[:], COPY)
-                nc.scalar.dma_start(out[rows, cols], plain[:])
+                if m == KEY:
+                    nc.scalar.activation(plain[:], y[:], COPY)
+                    nc.scalar.dma_start(out[rows, cols], plain[:])
+                else:
+                    nc.vector.tensor_copy(plain[:], y[:])
+                    nc.sync.dma_start(out[rows, cols], plain[:])

@@ -24,13 +24,13 @@ def tile_compressedllamaattention_kernel(tc, table, w, cos_t, sin_t, offs, out):
         tc.tile_pool(name="work", bufs=4) as work,
         tc.psum_pool(name="psum", bufs=8) as psum,
     ):
+        tokens = held.tile([P, S], BF16, name="tokens")
+        nc.sync.dma_start(tokens[:, : S // 2], table[:, : S // 2])
+        nc.scalar.dma_start(tokens[:, S // 2 :], table[:, S // 2 :])
         offsets = held.tile([P, N // 16], U16, name="offsets")
         nc.sync.dma_start(offsets[:], offs)
         weights = held.tile([P, M], BF16, name="weights")
         nc.scalar.dma_start(weights[:], w)
-        tokens = held.tile([P, S], BF16, name="tokens")
-        nc.sync.dma_start(tokens[:, : S // 2], table[:, : S // 2])
-        nc.scalar.dma_start(tokens[:, S // 2 :], table[:, S // 2 :])
         cosines = held.tile([P, N], F32, name="cosines")
         sines = held.tile([P, N], F32, name="sines")
         for p in range(PIECES):
@@ -60,20 +60,16 @@ def tile_compressedllamaattention_kernel(tc, table, w, cos_t, sin_t, offs, out):
                 partner_sin = work.tile([P, PIECE], F32, name="partner_sin")
                 nc.vector.tensor_tensor(partner_sin[:], partner[:], sines[:, cols], MULT)
                 rotated = work.tile([P, PIECE], F32, name="rotated")
-                nc.gpsimd.tensor_tensor(rotated[:], y_cos[:], partner_sin[:], ADD)
+                adder = nc.vector if (p == PIECES - 1 and h == HEADS_Q - 1) else nc.gpsimd
+                adder.tensor_tensor(rotated[:], y_cos[:], partner_sin[:], ADD)
                 nc.sync.dma_start(out[rows, cols], rotated[:])
 
-        KEY, VALUE = HEADS_Q, HEADS_Q + 1
         for p in range(PIECES):
             cols = slice(p * PIECE, (p + 1) * PIECE)
-            for m in (KEY, VALUE):
+            for m in range(HEADS_Q, M // P):
                 rows = slice(m * P, (m + 1) * P)
                 y = psum.tile([P, PIECE], F32, name="y", tag="bank")
                 nc.tensor.matmul(y[:], weights[:, rows], looked_up(p), start=True, stop=True)
                 plain = work.tile([P, PIECE], F32, name="plain")
-                if m == KEY:
-                    nc.scalar.activation(plain[:], y[:], COPY)
-                    nc.scalar.dma_start(out[rows, cols], plain[:])
-                else:
-                    nc.vector.tensor_copy(plain[:], y[:])
-                    nc.sync.dma_start(out[rows, cols], plain[:])
+                nc.scalar.activation(plain[:], y[:], COPY)
+                nc.scalar.dma_start(out[rows, cols], plain[:])

@@ -9,10 +9,10 @@ S = 4096
 N = 1024
 M = 512
 HEADS_Q = 2
+KEY, VALUE = 2, 3
 HALF = P // 2
 PIECE = 512
 PIECES = N // PIECE
-PIECE_COLS = PIECE // 16
 
 FLOPS = 2 * P * M * N
 
@@ -44,32 +44,37 @@ def tile_compressedllamaattention_kernel(tc, table, w, cos_t, sin_t, offs, out):
             nc.vector.tensor_scalar_mul(partner_weights[:, lo:mid], weights[:, mid:hi], -1.0)
             nc.vector.tensor_copy(partner_weights[:, mid:hi], weights[:, lo:mid])
 
-        def looked_up(p):
-            return tokens[:].indirect(offsets[:, p * PIECE_COLS : (p + 1) * PIECE_COLS])
+        def product(stationary, first, count):
+            bank = psum.tile([P, PIECE], F32, name="bank")
+            looked_up = tokens[:].indirect(offsets[:, first // 16 : (first + count) // 16])
+            nc.tensor.matmul(bank[:, :count], stationary, looked_up, start=True, stop=True)
+            return bank[:, :count]
 
-        for p in range(PIECES):
-            cols = slice(p * PIECE, (p + 1) * PIECE)
-            for h in range(HEADS_Q):
-                rows = slice(h * P, (h + 1) * P)
-                y = psum.tile([P, PIECE], F32, name="y", tag="bank")
-                nc.tensor.matmul(y[:], weights[:, rows], looked_up(p), start=True, stop=True)
-                partner = psum.tile([P, PIECE], F32, name="partner", tag="bank")
-                nc.tensor.matmul(partner[:], partner_weights[:, rows], looked_up(p), start=True, stop=True)
-                y_cos = work.tile([P, PIECE], F32, name="y_cos")
-                nc.vector.tensor_tensor(y_cos[:], y[:], cosines[:, cols], MULT)
-                partner_sin = work.tile([P, PIECE], F32, name="partner_sin")
-                nc.vector.tensor_tensor(partner_sin[:], partner[:], sines[:, cols], MULT)
-                rotated = work.tile([P, PIECE], F32, name="rotated")
-                adder = nc.vector if (p == PIECES - 1 and h == HEADS_Q - 1) else nc.gpsimd
-                adder.tensor_tensor(rotated[:], y_cos[:], partner_sin[:], ADD)
-                nc.sync.dma_start(out[rows, cols], rotated[:])
+        def query_head(h, first, count, adder):
+            rows = slice(h * P, (h + 1) * P)
+            cols = slice(first, first + count)
+            y = product(weights[:, rows], first, count)
+            partner = product(partner_weights[:, rows], first, count)
+            y_cos = work.tile([P, PIECE], F32, name="y_cos")
+            nc.vector.tensor_tensor(y_cos[:, :count], y, cosines[:, cols], MULT)
+            partner_sin = work.tile([P, PIECE], F32, name="partner_sin")
+            nc.vector.tensor_tensor(partner_sin[:, :count], partner, sines[:, cols], MULT)
+            rotated = work.tile([P, PIECE], F32, name="rotated")
+            adder.tensor_tensor(rotated[:, :count], y_cos[:, :count], partner_sin[:, :count], ADD)
+            nc.sync.dma_start(out[rows, cols], rotated[:, :count])
 
-        for p in range(PIECES):
-            cols = slice(p * PIECE, (p + 1) * PIECE)
-            for m in range(HEADS_Q, M // P):
-                rows = slice(m * P, (m + 1) * P)
-                y = psum.tile([P, PIECE], F32, name="y", tag="bank")
-                nc.tensor.matmul(y[:], weights[:, rows], looked_up(p), start=True, stop=True)
-                plain = work.tile([P, PIECE], F32, name="plain")
-                nc.scalar.activation(plain[:], y[:], COPY)
-                nc.scalar.dma_start(out[rows, cols], plain[:])
+        def plain_head(m, first, count):
+            rows = slice(m * P, (m + 1) * P)
+            y = product(weights[:, rows], first, count)
+            plain = work.tile([P, PIECE], F32, name="plain")
+            nc.scalar.activation(plain[:, :count], y, COPY)
+            nc.scalar.dma_start(out[rows, first : first + count], plain[:, :count])
+
+        query_head(0, 0, PIECE, nc.gpsimd)
+        plain_head(KEY, 0, PIECE)
+        query_head(1, 0, PIECE, nc.gpsimd)
+        plain_head(VALUE, 0, PIECE)
+        query_head(0, PIECE, PIECE, nc.gpsimd)
+        query_head(1, PIECE, PIECE, nc.vector)
+        plain_head(KEY, PIECE, PIECE)
+        plain_head(VALUE, PIECE, PIECE)

@@ -12,7 +12,6 @@ HEADS_Q = 2
 KEY, VALUE = 2, 3
 HALF = P // 2
 PIECE = 512
-PIECES = N // PIECE
 
 FLOPS = 2 * P * M * N
 
@@ -30,13 +29,15 @@ def tile_compressedllamaattention_kernel(tc, table, w, cos_t, sin_t, offs, out):
         offsets = held.tile([P, N // 16], U16, name="offsets")
         nc.sync.dma_start(offsets[:], offs)
         weights = held.tile([P, M], BF16, name="weights")
-        nc.scalar.dma_start(weights[:], w)
+        nc.scalar.dma_start(weights[:, :P], w[:, :P])
+        nc.scalar.dma_start(weights[:, P:], w[:, P:])
         cosines = held.tile([P, N], F32, name="cosines")
         sines = held.tile([P, N], F32, name="sines")
-        for p in range(PIECES):
-            cols = slice(p * PIECE, (p + 1) * PIECE)
-            nc.sync.dma_start(cosines[:, cols], cos_t[:, cols])
-            nc.scalar.dma_start(sines[:, cols], sin_t[:, cols])
+        first_piece, second_piece = slice(0, PIECE), slice(PIECE, N)
+        nc.sync.dma_start(cosines[:, first_piece], cos_t[:, first_piece])
+        nc.scalar.dma_start(sines[:, first_piece], sin_t[:, first_piece])
+        nc.sync.dma_start(cosines[:, second_piece], cos_t[:, second_piece])
+        nc.sync.dma_start(sines[:, second_piece], sin_t[:, second_piece])
 
         partner_weights = held.tile([P, HEADS_Q * P], BF16, name="partner_weights")
         for h in range(HEADS_Q):

@@ -12,6 +12,7 @@ HEADS_Q = 2
 KEY, VALUE = 2, 3
 HALF = P // 2
 PIECE = 512
+TAIL = PIECE // 2
 
 FLOPS = 2 * P * M * N
 
@@ -51,7 +52,7 @@ def tile_compressedllamaattention_kernel(tc, table, w, cos_t, sin_t, offs, out):
             nc.tensor.matmul(bank[:, :count], stationary, looked_up, start=True, stop=True)
             return bank[:, :count]
 
-        def query_head(h, first, count, adder):
+        def rotate(h, first, count, adder, rotated):
             rows = slice(h * P, (h + 1) * P)
             cols = slice(first, first + count)
             y = product(weights[:, rows], first, count)
@@ -60,22 +61,28 @@ def tile_compressedllamaattention_kernel(tc, table, w, cos_t, sin_t, offs, out):
             nc.vector.tensor_tensor(y_cos[:, :count], y, cosines[:, cols], MULT)
             partner_sin = work.tile([P, PIECE], F32, name="partner_sin")
             nc.vector.tensor_tensor(partner_sin[:, :count], partner, sines[:, cols], MULT)
+            adder.tensor_tensor(rotated, y_cos[:, :count], partner_sin[:, :count], ADD)
+
+        def query_head(h, first, chunk, adder):
             rotated = work.tile([P, PIECE], F32, name="rotated")
-            adder.tensor_tensor(rotated[:, :count], y_cos[:, :count], partner_sin[:, :count], ADD)
-            nc.sync.dma_start(out[rows, cols], rotated[:, :count])
+            for start in range(0, PIECE, chunk):
+                rotate(h, first + start, chunk, adder, rotated[:, start : start + chunk])
+            nc.sync.dma_start(out[h * P : (h + 1) * P, first : first + PIECE], rotated[:])
 
         def plain_head(m, first, count):
             rows = slice(m * P, (m + 1) * P)
-            y = product(weights[:, rows], first, count)
-            plain = work.tile([P, PIECE], F32, name="plain")
-            nc.scalar.activation(plain[:, :count], y, COPY)
-            nc.scalar.dma_start(out[rows, first : first + count], plain[:, :count])
+            plain = work.tile([P, count], F32, name=f"plain_{count}")
+            for start in range(0, count, PIECE):
+                chunk = min(PIECE, count - start)
+                y = product(weights[:, rows], first + start, chunk)
+                nc.scalar.activation(plain[:, start : start + chunk], y, COPY)
+            nc.scalar.dma_start(out[rows, first : first + count], plain[:])
 
         query_head(0, 0, PIECE, nc.gpsimd)
         plain_head(KEY, 0, PIECE)
         query_head(1, 0, PIECE, nc.gpsimd)
-        plain_head(VALUE, 0, PIECE)
+        plain_head(VALUE, 0, N - TAIL)
         query_head(0, PIECE, PIECE, nc.gpsimd)
-        query_head(1, PIECE, PIECE, nc.vector)
         plain_head(KEY, PIECE, PIECE)
-        plain_head(VALUE, PIECE, PIECE)
+        query_head(1, PIECE, TAIL, nc.vector)
+        plain_head(VALUE, N - TAIL, TAIL)

import concourse.mybir as mybir

BF16, F32, U16 = mybir.dt.bfloat16, mybir.dt.float32, mybir.dt.uint16
MULT, ADD = mybir.AluOpType.mult, mybir.AluOpType.add
COPY = mybir.ActivationFunctionType.Copy

P = 128
S = 4096
N = 1024
M = 512
HEADS_Q = 2
KEY, VALUE = 2, 3
HALF = P // 2
PIECE = 512
TAIL = PIECE // 2

FLOPS = 2 * P * M * N


def tile_compressedllamaattention_kernel(tc, table, w, cos_t, sin_t, offs, out):
    nc = tc.nc
    with (
        tc.tile_pool(name="held", bufs=1) as held,
        tc.tile_pool(name="work", bufs=4) as work,
        tc.psum_pool(name="psum", bufs=8) as psum,
    ):
        tokens = held.tile([P, S], BF16, name="tokens")
        nc.sync.dma_start(tokens[:, : S // 2], table[:, : S // 2])
        nc.scalar.dma_start(tokens[:, S // 2 :], table[:, S // 2 :])
        offsets = held.tile([P, N // 16], U16, name="offsets")
        nc.sync.dma_start(offsets[:], offs)
        weights = held.tile([P, M], BF16, name="weights")
        nc.scalar.dma_start(weights[:, :P], w[:, :P])
        nc.scalar.dma_start(weights[:, P:], w[:, P:])
        cosines = held.tile([P, N], F32, name="cosines")
        sines = held.tile([P, N], F32, name="sines")
        first_piece, second_piece = slice(0, PIECE), slice(PIECE, N)
        nc.sync.dma_start(cosines[:, first_piece], cos_t[:, first_piece])
        nc.scalar.dma_start(sines[:, first_piece], sin_t[:, first_piece])
        nc.sync.dma_start(cosines[:, second_piece], cos_t[:, second_piece])
        nc.sync.dma_start(sines[:, second_piece], sin_t[:, second_piece])

        partner_weights = held.tile([P, HEADS_Q * P], BF16, name="partner_weights")
        for h in range(HEADS_Q):
            lo, mid, hi = h * P, h * P + HALF, (h + 1) * P
            nc.vector.tensor_scalar_mul(partner_weights[:, lo:mid], weights[:, mid:hi], -1.0)
            nc.vector.tensor_copy(partner_weights[:, mid:hi], weights[:, lo:mid])

        def product(stationary, first, count):
            bank = psum.tile([P, PIECE], F32, name="bank")
            looked_up = tokens[:].indirect(offsets[:, first // 16 : (first + count) // 16])
            nc.tensor.matmul(bank[:, :count], stationary, looked_up, start=True, stop=True)
            return bank[:, :count]

        def rotate(h, first, count, adder, rotated):
            rows = slice(h * P, (h + 1) * P)
            cols = slice(first, first + count)
            y = product(weights[:, rows], first, count)
            partner = product(partner_weights[:, rows], first, count)
            y_cos = work.tile([P, PIECE], F32, name="y_cos")
            nc.vector.tensor_tensor(y_cos[:, :count], y, cosines[:, cols], MULT)
            partner_sin = work.tile([P, PIECE], F32, name="partner_sin")
            nc.vector.tensor_tensor(partner_sin[:, :count], partner, sines[:, cols], MULT)
            adder.tensor_tensor(rotated, y_cos[:, :count], partner_sin[:, :count], ADD)

        def query_head(h, first, chunk, adder):
            rotated = work.tile([P, PIECE], F32, name="rotated")
            for start in range(0, PIECE, chunk):
                rotate(h, first + start, chunk, adder, rotated[:, start : start + chunk])
            nc.sync.dma_start(out[h * P : (h + 1) * P, first : first + PIECE], rotated[:])

        def plain_head(m, first, count):
            rows = slice(m * P, (m + 1) * P)
            plain = work.tile([P, count], F32, name=f"plain_{count}")
            for start in range(0, count, PIECE):
                chunk = min(PIECE, count - start)
                y = product(weights[:, rows], first + start, chunk)
                nc.scalar.activation(plain[:, start : start + chunk], y, COPY)
            nc.scalar.dma_start(out[rows, first : first + count], plain[:])

        query_head(0, 0, PIECE, nc.gpsimd)
        plain_head(KEY, 0, PIECE)
        query_head(1, 0, PIECE, nc.gpsimd)
        plain_head(VALUE, 0, N - TAIL)
        query_head(0, PIECE, PIECE, nc.gpsimd)
        plain_head(KEY, PIECE, PIECE)
        query_head(1, PIECE, TAIL, nc.vector)
        plain_head(VALUE, N - TAIL, TAIL)
